import numpy as np
import ml_dtypes


def mxq(x, axis, fmt="e4m3"):
    dtype, down = {"e4m3": (ml_dtypes.float8_e4m3fn, 7), "e5m2": (ml_dtypes.float8_e5m2, 14)}[fmt]
    v = np.moveaxis(np.asarray(x, np.float32).astype(ml_dtypes.bfloat16).astype(np.float64), axis, -1)
    blocks = v.reshape(v.shape[:-1] + (-1, 32))
    amax = np.abs(blocks).max(-1, keepdims=True)
    byte = np.maximum(np.where(amax > 0, np.frexp(amax)[1] - 1 + 127, 0) - down, 1)
    scale = np.exp2(byte - 127.0)
    codes = (blocks / scale).astype(np.float32).astype(dtype).astype(np.float64)
    return np.moveaxis((codes * scale).reshape(v.shape), -1, axis)


WIDE = False


def mx_kscale(k):
    if not WIDE:
        return np.ones(k)
    levels = np.array([10, -10, 5, -5, 0])
    a = np.random.permutation(np.resize(levels, k // 512 * 4)).reshape(k // 512, 4)
    idx = np.arange(k)
    return np.exp2(a[idx // 512, idx % 128 // 32])


BF16 = ml_dtypes.bfloat16


def bf(x):
    return np.asarray(x, np.float32).astype(BF16)


def f64(x):
    return np.asarray(x).astype(np.float64)


B, I, H, ORDER = 256, 8192, 512, 3
OH = ORDER * H


def sigmoid(v):
    return 1.0 / (1.0 + np.exp(-v))


def setup_inputs():
    s, t = mx_kscale(I), mx_kscale(OH)
    return {"x": bf(np.random.standard_normal((B, I)) * s),
            "me_output": bf(np.random.standard_normal((B, OH)) * t),
            "W_memi": bf(np.random.standard_normal((I, OH)) * 0.7 / np.sqrt(I) / s[:, None]),
            "W_memh": bf(np.random.standard_normal((OH, OH)) * 0.7 / np.sqrt(OH) / t[:, None]),
            "W_memt": bf(np.random.standard_normal((OH, H)) * 1.0 / np.sqrt(OH) / t[:, None]),
            "mem_bias": bf(np.random.standard_normal(OH) * 0.3)}


def reference(x, me_output, W_memi, W_memh, W_memt, mem_bias):
    me = f64(me_output)
    mg = ((mxq(f64(x), 1, "e4m3") @ mxq(f64(W_memi), 0, "e4m3"))
          + (mxq(me, 1, "e4m3") @ mxq(f64(W_memh), 0, "e4m3"))
          + f64(mem_bias))
    gated = sigmoid(mg) * me
    return mxq(gated, 1, "e4m3") @ mxq(f64(W_memt), 0, "e4m3")

@@ -1,0 +1,240 @@
+import concourse.mybir as mybir
+from concourse.masks import make_identity
+
+F32 = mybir.dt.float32
+BF16 = mybir.dt.bfloat16
+U32 = mybir.dt.uint32
+U8 = mybir.dt.uint8
+FP8X4 = mybir.dt.float8_e4m3fn_x4
+ADD = mybir.AluOpType.add
+MULT = mybir.AluOpType.mult
+SIGMOID = mybir.ActivationFunctionType.Sigmoid
+
+B, I, OH, H = 256, 8192, 1536, 512
+FLOPS = 2 * B * (I * OH + OH * OH + OH * H)
+
+P = 128
+PACK = 4
+K_PASS = P * PACK
+N_BLOCK = 512
+B_TILES = B // P
+
+X_PASSES = I // K_PASS
+ME_PASSES = OH // K_PASS
+PASSES = X_PASSES + ME_PASSES
+COL_BLOCKS = OH // N_BLOCK
+
+BLOCKS_PER_RAW = 3
+RAW_TILES = X_PASSES + COL_BLOCKS + 1
+BLOCKS = RAW_TILES * BLOCKS_PER_RAW
+
+SLAB_PASSES = 4
+LOAD_AHEAD = 5
+ACT_LEAD = 3
+LAG = 2
+
+
+def tile_lstmcell_pa_k_kernel(tc, x, me_output, W_memi, W_memh, W_memt, mem_bias, out):
+    nc = tc.nc
+    with (
+        tc.tile_pool(name="const", bufs=1) as const,
+        tc.tile_pool(name="slabs", bufs=X_PASSES // SLAB_PASSES) as slabs,
+        tc.tile_pool(name="raws", bufs=LOAD_AHEAD + 1) as raws,
+        tc.tile_pool(name="stream", bufs=5) as stream,
+        tc.tile_pool(name="gate", bufs=3) as gate_pool,
+        tc.psum_pool(name="sums", bufs=B_TILES * COL_BLOCKS) as sums,
+        tc.psum_pool(name="turn", bufs=2) as turn,
+    ):
+        ident_f32 = const.tile([P, P], F32)
+        make_identity(nc, ident_f32[:])
+        ident_bf16 = const.tile([P, P], BF16)
+        make_identity(nc, ident_bf16[:])
+
+        warm = const.tile([P, 1], F32)
+        nc.vector.memset(warm[:], 0.0)
+        nc.scalar.activation(out=warm[:], in_=warm[:], func=SIGMOID)
+
+        ones = const.tile([P, P], BF16)
+        nc.vector.memset(ones[:], 1.0)
+        bias_rows = const.tile([P, OH], BF16)
+        nc.vector.memset(bias_rows[:], 0.0)
+        nc.scalar.dma_start(out=bias_rows[0:1, :], in_=mem_bias.rearrange("(o n) -> o n", o=1))
+        bias_all = const.tile([P, OH], F32)
+        for cb in range(COL_BLOCKS):
+            cols = slice(cb * N_BLOCK, (cb + 1) * N_BLOCK)
+            spread = turn.tile([P, N_BLOCK], F32, tag="turn")
+            nc.tensor.matmul(out=spread[:], lhsT=ones[:], rhs=bias_rows[:, cols], start=True, stop=True)
+            nc.vector.tensor_copy(out=bias_all[:, cols], in_=spread[:])
+
+        act_codes = const.tile([P, PASSES, B], U32, align_bytes=64)
+        act_scales = const.tile([P, PASSES, B], U8, align_bytes=64)
+        gated_codes = const.tile([P, ME_PASSES, B], U32, align_bytes=64)
+        gated_scales = const.tile([P, ME_PASSES, B], U8, align_bytes=64)
+        me_rows = [const.tile([P, OH], BF16, name="me_rows%d" % bt) for bt in range(B_TILES)]
+        x_slabs = []
+        raw_tiles = []
+        grouped_tiles = []
+        mg = [
+            [sums.tile([P, N_BLOCK], F32, tag="sum", name="mg%d_%d" % (bt, cb)) for cb in range(COL_BLOCKS)]
+            for bt in range(B_TILES)
+        ]
+        out_sums = []
+
+        def load_activations(s):
+            for bt in range(B_TILES):
+                rows = slice(bt * P, (bt + 1) * P)
+                if s < X_PASSES // SLAB_PASSES:
+                    if bt == 0:
+                        x_slabs.append([])
+                    slab = slabs.tile([P, SLAB_PASSES * K_PASS], BF16, tag="slab%d" % bt, name="slab%d" % bt)
+                    width = SLAB_PASSES * K_PASS
+                    nc.sync.dma_start(out=slab[:], in_=x[rows, s * width : (s + 1) * width])
+                    x_slabs[s].append(slab)
+                else:
+                    nc.sync.dma_start(out=me_rows[bt][:], in_=me_output[rows, :])
+
+        def load_raw(r):
+            g = r + ACT_LEAD
+            if g < PASSES and g % SLAB_PASSES == 0:
+                load_activations(g // SLAB_PASSES)
+            raw = raws.tile([P, BLOCKS_PER_RAW * PACK * N_BLOCK], BF16, tag="raw", name="raw")
+            if r < X_PASSES:
+                nc.sync.dma_start(
+                    out=raw[:].rearrange("q (u ec) -> q u ec", u=2),
+                    in_=W_memi[r * K_PASS : (r + 1) * K_PASS, :].rearrange("(u q e) c -> q u (e c)", u=2, e=2),
+                )
+            else:
+                if r < X_PASSES + COL_BLOCKS:
+                    cb = r - X_PASSES
+                    source = W_memh[:, cb * N_BLOCK : (cb + 1) * N_BLOCK]
+                else:
+                    source = W_memt
+                nc.sync.dma_start(
+                    out=raw[:].rearrange("p (gt c) -> p gt c", c=N_BLOCK),
+                    in_=source.rearrange("(gt p) c -> p gt c", p=P),
+                )
+            raw_tiles.append(raw)
+
+        def block_source(r, i):
+            if r < X_PASSES:
+                return raw_tiles[r][:].rearrange("q (t c) -> q t c", t=PACK)[:, :, i * N_BLOCK : (i + 1) * N_BLOCK]
+            return raw_tiles[r][:].rearrange("p (g t c) -> p g t c", t=PACK, c=N_BLOCK)[:, i, :, :]
+
+        def pack_planes(rows, grouped):
+            planes = turn.tile([P, PACK, P], BF16, tag="turn", name="planes")
+            for t in range(PACK):
+                nc.tensor.transpose(planes[:, t, :], rows[:, t * P : (t + 1) * P], ident_bf16[:])
+            nc.scalar.copy(out=grouped, in_=planes[:].rearrange("p t b -> p b t"))
+
+        def pack_words(s, local, grouped):
+            words = turn.tile([P, B_TILES, 2, P], F32, tag="turn", name="words")
+            for bt in range(B_TILES):
+                as_words = x_slabs[s][bt][:].bitcast(F32)
+                for u in range(2):
+                    first = (2 * local + u) * P
+                    nc.tensor.transpose(words[:, bt, u, :], as_words[:, first : first + P], ident_f32[:])
+            nc.scalar.copy(out=grouped.bitcast(F32), in_=words[:].rearrange("q a u b -> q a b u"))
+
+        def prepare_activations(g):
+            grouped = stream.tile([P, B_TILES, P, PACK], BF16, tag="act_grouped", name="act_grouped", align_bytes=64)
+            if g < X_PASSES:
+                pack_words(g // SLAB_PASSES, g % SLAB_PASSES, grouped[:])
+            else:
+                first = (g - X_PASSES) * K_PASS
+                for bt in range(B_TILES):
+                    pack_planes(me_rows[bt][:, first : first + K_PASS], grouped[:, bt, :, :])
+            nc.vector.quantize_mx(
+                out=act_codes[:, g, :].bitcast(FP8X4),
+                scales=act_scales[:, g, :],
+                in_=grouped[:].rearrange("p a b t -> p (a b t)"),
+            )
+
+        def regroup(j):
+            source = block_source(j // BLOCKS_PER_RAW, j % BLOCKS_PER_RAW)
+            grouped = stream.tile([P, N_BLOCK, PACK], BF16, tag="grouped", name="grouped", align_bytes=64)
+            dst = grouped[:].rearrange("p (c i) t -> p c t i", i=4)
+            src = source.rearrange("p t (c i) -> p c t i", i=4)
+            if j % 2 == 0:
+                nc.vector.tensor_copy(out=dst, in_=src)
+            else:
+                nc.scalar.copy(out=dst, in_=src)
+            grouped_tiles.append(grouped)
+
+        def multiply(sum_tiles, codes_of_pass, scales_of_pass, codes, scales, start, stop):
+            for bt in range(B_TILES):
+                rows = slice(bt * P, (bt + 1) * P)
+                nc.tensor.matmul_mx(
+                    out=sum_tiles[bt][:],
+                    lhsT=codes_of_pass[:, rows].bitcast(FP8X4),
+                    lhsT_scale=scales_of_pass[:, rows],
+                    rhs=codes[:].bitcast(FP8X4),
+                    rhs_scale=scales[:],
+                    start=start,
+                    stop=stop,
+                )
+
+        def gate(cb):
+            cols = slice(cb * N_BLOCK, (cb + 1) * N_BLOCK)
+            grouped = gate_pool.tile([P, B_TILES, P, PACK], BF16, tag="gated_grouped", name="gated_grouped", align_bytes=64)
+            for bt in range(B_TILES):
+                z = gate_pool.tile([P, N_BLOCK], F32, tag="z", name="z")
+                nc.vector.tensor_tensor(out=z[:], in0=mg[bt][cb][:], in1=bias_all[:, cols], op=ADD)
+                nc.scalar.activation(out=z[:], in_=z[:], func=SIGMOID)
+                gated = gate_pool.tile([P, N_BLOCK], BF16, tag="gated", name="gated")
+                nc.vector.tensor_tensor(out=gated[:], in0=z[:], in1=me_rows[bt][:, cols], op=MULT)
+                pack_planes(gated[:], grouped[:, bt, :, :])
+            nc.vector.quantize_mx(
+                out=gated_codes[:, cb, :].bitcast(FP8X4),
+                scales=gated_scales[:, cb, :],
+                in_=grouped[:].rearrange("p a b t -> p (a b t)"),
+            )
+
+        def finish(j):
+            r, i = divmod(j, BLOCKS_PER_RAW)
+            codes = stream.tile([P, N_BLOCK], U32, tag="codes", name="codes", align_bytes=64)
+            scales = stream.tile([P, N_BLOCK], U8, tag="scales", name="scales", align_bytes=64)
+            nc.vector.quantize_mx(
+                out=codes[:].bitcast(FP8X4),
+                scales=scales[:],
+                in_=grouped_tiles[j][:].rearrange("p c t -> p (c t)"),
+            )
+            if r < X_PASSES:
+                column = [mg[bt][i] for bt in range(B_TILES)]
+                multiply(column, act_codes[:, r, :], act_scales[:, r, :], codes, scales, r == 0, False)
+            elif r < X_PASSES + COL_BLOCKS:
+                cb = r - X_PASSES
+                g = X_PASSES + i
+                column = [mg[bt][cb] for bt in range(B_TILES)]
+                multiply(column, act_codes[:, g, :], act_scales[:, g, :], codes, scales, False, i == ME_PASSES - 1)
+                if i == ME_PASSES - 1:
+                    gate(cb)
+            else:
+                if i == 0:
+                    for bt in range(B_TILES):
+                        out_sums.append(sums.tile([P, H], F32, tag="sum", name="out_sum%d" % bt))
+                multiply(out_sums, gated_codes[:, i, :], gated_scales[:, i, :], codes, scales, i == 0, i == ME_PASSES - 1)
+
+        load_activations(0)
+        for r in range(LOAD_AHEAD):
+            load_raw(r)
+        for g in range(ACT_LEAD):
+            prepare_activations(g)
+        for j in range(BLOCKS + LAG):
+            if j < BLOCKS:
+                r = j // BLOCKS_PER_RAW
+                if j % BLOCKS_PER_RAW == 0:
+                    if r + LOAD_AHEAD < RAW_TILES:
+                        load_raw(r + LOAD_AHEAD)
+                    if r + ACT_LEAD < PASSES:
+                        prepare_activations(r + ACT_LEAD)
+                regroup(j)
+            if j >= LAG:
+                finish(j - LAG)
+
+        for bt in range(B_TILES):
+            result = gate_pool.tile([P, H], F32, tag="result", name="result")
+            if bt == 0:
+                nc.scalar.copy(out=result[:], in_=out_sums[bt][:])
+            else:
+                nc.vector.tensor_copy(out=result[:], in_=out_sums[bt][:])
+            nc.sync.dma_start(out=out[bt * P : (bt + 1) * P, :], in_=result[:])

@@ -27,10 +27,14 @@ COL_BLOCKS = OH // N_BLOCK
 BLOCKS_PER_RAW = 3
 RAW_TILES = X_PASSES + COL_BLOCKS + 1
 BLOCKS = RAW_TILES * BLOCKS_PER_RAW
+FIRST_MEMORY_BLOCK = X_PASSES * BLOCKS_PER_RAW
 
 SLAB_PASSES = 4
+X_SLABS = X_PASSES // SLAB_PASSES
 LOAD_AHEAD = 5
-ACT_LEAD = 3
+TURN_LEAD = 4
+COLLECT_LEAD = 2
+SLAB_LEAD = 3
 LAG = 2
 
 
@@ -38,12 +42,13 @@ def tile_lstmcell_pa_k_kernel(tc, x, me_output, W_memi, W_memh, W_memt, mem_bias
     nc = tc.nc
     with (
         tc.tile_pool(name="const", bufs=1) as const,
-        tc.tile_pool(name="slabs", bufs=X_PASSES // SLAB_PASSES) as slabs,
+        tc.tile_pool(name="slabs", bufs=3) as slabs,
         tc.tile_pool(name="raws", bufs=LOAD_AHEAD + 1) as raws,
-        tc.tile_pool(name="stream", bufs=5) as stream,
-        tc.tile_pool(name="gate", bufs=3) as gate_pool,
+        tc.tile_pool(name="stream", bufs=6) as stream,
+        tc.tile_pool(name="gate", bufs=4) as gate_pool,
         tc.psum_pool(name="sums", bufs=B_TILES * COL_BLOCKS) as sums,
         tc.psum_pool(name="turn", bufs=2) as turn,
+        tc.manual_schedule(),
     ):
         ident_f32 = const.tile([P, P], F32)
         make_identity(nc, ident_f32[:])
@@ -54,36 +59,28 @@ def tile_lstmcell_pa_k_kernel(tc, x, me_output, W_memi, W_memh, W_memt, mem_bias
         nc.vector.memset(warm[:], 0.0)
         nc.scalar.activation(out=warm[:], in_=warm[:], func=SIGMOID)
 
-        ones = const.tile([P, P], BF16)
-        nc.vector.memset(ones[:], 1.0)
-        bias_rows = const.tile([P, OH], BF16)
-        nc.vector.memset(bias_rows[:], 0.0)
-        nc.scalar.dma_start(out=bias_rows[0:1, :], in_=mem_bias.rearrange("(o n) -> o n", o=1))
-        bias_all = const.tile([P, OH], F32)
-        for cb in range(COL_BLOCKS):
-            cols = slice(cb * N_BLOCK, (cb + 1) * N_BLOCK)
-            spread = turn.tile([P, N_BLOCK], F32, tag="turn")
-            nc.tensor.matmul(out=spread[:], lhsT=ones[:], rhs=bias_rows[:, cols], start=True, stop=True)
-            nc.vector.tensor_copy(out=bias_all[:, cols], in_=spread[:])
-
+        bias_all = const.tile([P, OH], BF16)
         act_codes = const.tile([P, PASSES, B], U32, align_bytes=64)
         act_scales = const.tile([P, PASSES, B], U8, align_bytes=64)
         gated_codes = const.tile([P, ME_PASSES, B], U32, align_bytes=64)
         gated_scales = const.tile([P, ME_PASSES, B], U8, align_bytes=64)
+        read_codes = const.tile([P, ME_PASSES, H], U32, align_bytes=64)
+        read_scales = const.tile([P, ME_PASSES, H], U8, align_bytes=64)
         me_rows = [const.tile([P, OH], BF16, name="me_rows%d" % bt) for bt in range(B_TILES)]
         x_slabs = []
         raw_tiles = []
         grouped_tiles = []
+        turned = {}
+        act_grouped = {}
         mg = [
             [sums.tile([P, N_BLOCK], F32, tag="sum", name="mg%d_%d" % (bt, cb)) for cb in range(COL_BLOCKS)]
             for bt in range(B_TILES)
         ]
-        out_sums = []
 
         def load_activations(s):
             for bt in range(B_TILES):
                 rows = slice(bt * P, (bt + 1) * P)
-                if s < X_PASSES // SLAB_PASSES:
+                if s < X_SLABS:
                     if bt == 0:
                         x_slabs.append([])
                     slab = slabs.tile([P, SLAB_PASSES * K_PASS], BF16, tag="slab%d" % bt, name="slab%d" % bt)
@@ -92,26 +89,35 @@ def tile_lstmcell_pa_k_kernel(tc, x, me_output, W_memi, W_memh, W_memt, mem_bias
                     x_slabs[s].append(slab)
                 else:
                     nc.sync.dma_start(out=me_rows[bt][:], in_=me_output[rows, :])
+            if s == X_SLABS:
+                nc.sync.dma_start(out=bias_all[:], in_=mem_bias.partition_broadcast(P))
 
         def load_raw(r):
-            g = r + ACT_LEAD
-            if g < PASSES and g % SLAB_PASSES == 0:
-                load_activations(g // SLAB_PASSES)
+            if r + SLAB_LEAD < PASSES and (r + SLAB_LEAD) % SLAB_PASSES == 0:
+                load_activations((r + SLAB_LEAD) // SLAB_PASSES)
             raw = raws.tile([P, BLOCKS_PER_RAW * PACK * N_BLOCK], BF16, tag="raw", name="raw")
             if r < X_PASSES:
-                nc.sync.dma_start(
-                    out=raw[:].rearrange("q (u ec) -> q u ec", u=2),
-                    in_=W_memi[r * K_PASS : (r + 1) * K_PASS, :].rearrange("(u q e) c -> q u (e c)", u=2, e=2),
-                )
+                rows_of_pass = W_memi[r * K_PASS : (r + 1) * K_PASS, :].rearrange("(q t) c -> q t c", t=PACK)
+                pieces = BLOCKS_PER_RAW if r == 0 else 1
+                width = OH // pieces
+                for piece in range(pieces):
+                    cols = slice(piece * width, (piece + 1) * width)
+                    nc.sync.dma_start(
+                        out=raw[:].rearrange("q (t c) -> q t c", t=PACK)[:, :, cols], in_=rows_of_pass[:, :, cols]
+                    )
+            elif r < X_PASSES + COL_BLOCKS:
+                cb = r - X_PASSES
+                for g in range(ME_PASSES):
+                    nc.sync.dma_start(
+                        out=raw[:].rearrange("q (g t c) -> q g t c", t=PACK, c=N_BLOCK)[:, g, :, :],
+                        in_=W_memh[g * K_PASS : (g + 1) * K_PASS, cb * N_BLOCK : (cb + 1) * N_BLOCK].rearrange(
+                            "(q t) c -> q t c", t=PACK
+                        ),
+                    )
             else:
-                if r < X_PASSES + COL_BLOCKS:
-                    cb = r - X_PASSES
-                    source = W_memh[:, cb * N_BLOCK : (cb + 1) * N_BLOCK]
-                else:
-                    source = W_memt
                 nc.sync.dma_start(
                     out=raw[:].rearrange("p (gt c) -> p gt c", c=N_BLOCK),
-                    in_=source.rearrange("(gt p) c -> p gt c", p=P),
+                    in_=W_memt.rearrange("(gt p) c -> p gt c", p=P),
                 )
             raw_tiles.append(raw)
 
@@ -120,38 +126,33 @@ def tile_lstmcell_pa_k_kernel(tc, x, me_output, W_memi, W_memh, W_memt, mem_bias
                 return raw_tiles[r][:].rearrange("q (t c) -> q t c", t=PACK)[:, :, i * N_BLOCK : (i + 1) * N_BLOCK]
             return raw_tiles[r][:].rearrange("p (g t c) -> p g t c", t=PACK, c=N_BLOCK)[:, i, :, :]
 
-        def pack_planes(rows, grouped):
-            planes = turn.tile([P, PACK, P], BF16, tag="turn", name="planes")
-            for t in range(PACK):
-                nc.tensor.transpose(planes[:, t, :], rows[:, t * P : (t + 1) * P], ident_bf16[:])
-            nc.scalar.copy(out=grouped, in_=planes[:].rearrange("p t b -> p b t"))
-
-        def pack_words(s, local, grouped):
+        def turn_activations(g):
+            if g < X_PASSES:
+                row_tiles, local = x_slabs[g // SLAB_PASSES], g % SLAB_PASSES
+            else:
+                row_tiles, local = me_rows, g - X_PASSES
             words = turn.tile([P, B_TILES, 2, P], F32, tag="turn", name="words")
             for bt in range(B_TILES):
-                as_words = x_slabs[s][bt][:].bitcast(F32)
+                as_words = row_tiles[bt][:].bitcast(F32).rearrange("b (q u) -> b q u", u=2)
                 for u in range(2):
-                    first = (2 * local + u) * P
-                    nc.tensor.transpose(words[:, bt, u, :], as_words[:, first : first + P], ident_f32[:])
-            nc.scalar.copy(out=grouped.bitcast(F32), in_=words[:].rearrange("q a u b -> q a b u"))
+                    nc.tensor.transpose(words[:, bt, u, :], as_words[:, local * P : (local + 1) * P, u], ident_f32[:])
+            turned[g] = words
 
-        def prepare_activations(g):
-            grouped = stream.tile([P, B_TILES, P, PACK], BF16, tag="act_grouped", name="act_grouped", align_bytes=64)
-            if g < X_PASSES:
-                pack_words(g // SLAB_PASSES, g % SLAB_PASSES, grouped[:])
-            else:
-                first = (g - X_PASSES) * K_PASS
-                for bt in range(B_TILES):
-                    pack_planes(me_rows[bt][:, first : first + K_PASS], grouped[:, bt, :, :])
+        def collect_activations(g):
+            grouped = stream.tile([P, B_TILES, P, PACK], BF16, tag="act_grouped", name="act_grouped", bufs=3, align_bytes=64)
+            nc.scalar.copy(out=grouped[:].bitcast(F32), in_=turned[g][:].rearrange("q a u b -> q a b u"))
+            act_grouped[g] = grouped
+
+        def quantise_activations(g):
             nc.vector.quantize_mx(
                 out=act_codes[:, g, :].bitcast(FP8X4),
                 scales=act_scales[:, g, :],
-                in_=grouped[:].rearrange("p a b t -> p (a b t)"),
+                in_=act_grouped[g][:].rearrange("p a b t -> p (a b t)"),
             )
 
         def regroup(j):
             source = block_source(j // BLOCKS_PER_RAW, j % BLOCKS_PER_RAW)
-            grouped = stream.tile([P, N_BLOCK, PACK], BF16, tag="grouped", name="grouped", align_bytes=64)
+            grouped = stream.tile([P, N_BLOCK, PACK], BF16, tag="grouped", name="grouped", bufs=8, align_bytes=64)
             dst = grouped[:].rearrange("p (c i) t -> p c t i", i=4)
             src = source.rearrange("p t (c i) -> p c t i", i=4)
             if j % 2 == 0:
@@ -167,36 +168,22 @@ def tile_lstmcell_pa_k_kernel(tc, x, me_output, W_memi, W_memh, W_memt, mem_bias
                     out=sum_tiles[bt][:],
                     lhsT=codes_of_pass[:, rows].bitcast(FP8X4),
                     lhsT_scale=scales_of_pass[:, rows],
-                    rhs=codes[:].bitcast(FP8X4),
-                    rhs_scale=scales[:],
+                    rhs=codes.bitcast(FP8X4),
+                    rhs_scale=scales,
                     start=start,
                     stop=stop,
                 )
 
-        def gate(cb):
-            cols = slice(cb * N_BLOCK, (cb + 1) * N_BLOCK)
-            grouped = gate_pool.tile([P, B_TILES, P, PACK], BF16, tag="gated_grouped", name="gated_grouped", align_bytes=64)
-            for bt in range(B_TILES):
-                z = gate_pool.tile([P, N_BLOCK], F32, tag="z", name="z")
-                nc.vector.tensor_tensor(out=z[:], in0=mg[bt][cb][:], in1=bias_all[:, cols], op=ADD)
-                nc.scalar.activation(out=z[:], in_=z[:], func=SIGMOID)
-                gated = gate_pool.tile([P, N_BLOCK], BF16, tag="gated", name="gated")
-                nc.vector.tensor_tensor(out=gated[:], in0=z[:], in1=me_rows[bt][:, cols], op=MULT)
-                pack_planes(gated[:], grouped[:, bt, :, :])
-            nc.vector.quantize_mx(
-                out=gated_codes[:, cb, :].bitcast(FP8X4),
-                scales=gated_scales[:, cb, :],
-                in_=grouped[:].rearrange("p a b t -> p (a b t)"),
-            )
-
         def finish(j):
             r, i = divmod(j, BLOCKS_PER_RAW)
-            codes = stream.tile([P, N_BLOCK], U32, tag="codes", name="codes", align_bytes=64)
-            scales = stream.tile([P, N_BLOCK], U8, tag="scales", name="scales", align_bytes=64)
+            if r < X_PASSES + COL_BLOCKS:
+                codes = stream.tile([P, N_BLOCK], U32, tag="codes", name="codes", align_bytes=64)[:]
+                scales = stream.tile([P, N_BLOCK], U8, tag="scales", name="scales", align_bytes=64)[:]
+            else:
+                codes = read_codes[:, i, :]
+                scales = read_scales[:, i, :]
             nc.vector.quantize_mx(
-                out=codes[:].bitcast(FP8X4),
-                scales=scales[:],
-                in_=grouped_tiles[j][:].rearrange("p c t -> p (c t)"),
+                out=codes.bitcast(FP8X4), scales=scales, in_=grouped_tiles[j][:].rearrange("p c t -> p (c t)")
             )
             if r < X_PASSES:
                 column = [mg[bt][i] for bt in range(B_TILES)]
@@ -206,33 +193,78 @@ def tile_lstmcell_pa_k_kernel(tc, x, me_output, W_memi, W_memh, W_memt, mem_bias
                 g = X_PASSES + i
                 column = [mg[bt][cb] for bt in range(B_TILES)]
                 multiply(column, act_codes[:, g, :], act_scales[:, g, :], codes, scales, False, i == ME_PASSES - 1)
-                if i == ME_PASSES - 1:
-                    gate(cb)
-            else:
-                if i == 0:
-                    for bt in range(B_TILES):
-                        out_sums.append(sums.tile([P, H], F32, tag="sum", name="out_sum%d" % bt))
-                multiply(out_sums, gated_codes[:, i, :], gated_scales[:, i, :], codes, scales, i == 0, i == ME_PASSES - 1)
+
+        z_tiles = {}
+        gated_planes = {}
+        gated_grouped = {}
+
+        def add_bias(cb):
+            cols = slice(cb * N_BLOCK, (cb + 1) * N_BLOCK)
+            for bt in range(B_TILES):
+                z = gate_pool.tile([P, N_BLOCK], F32, tag="z", name="z")
+                nc.vector.tensor_tensor(out=z[:], in0=mg[bt][cb][:], in1=bias_all[:, cols], op=ADD)
+                z_tiles[(cb, bt)] = z
+
+        def squash(cb):
+            for bt in range(B_TILES):
+                z = z_tiles[(cb, bt)]
+                nc.scalar.activation(out=z[:], in_=z[:], func=SIGMOID)
+
+        def mask_and_turn(cb):
+            cols = slice(cb * N_BLOCK, (cb + 1) * N_BLOCK)
+            for bt in range(B_TILES):
+                gated = gate_pool.tile([P, N_BLOCK], BF16, tag="gated", name="gated")
+                nc.vector.tensor_tensor(out=gated[:], in0=z_tiles[(cb, bt)][:], in1=me_rows[bt][:, cols], op=MULT)
+                planes = turn.tile([P, PACK, P], BF16, tag="turn", name="planes")
+                for t in range(PACK):
+                    nc.tensor.transpose(planes[:, t, :], gated[:, t * P : (t + 1) * P], ident_bf16[:])
+                gated_planes[(cb, bt)] = planes
+
+        def collect(cb):
+            grouped = gate_pool.tile([P, B_TILES, P, PACK], BF16, tag="gated_grouped", name="gated_grouped", bufs=2, align_bytes=64)
+            for bt in range(B_TILES):
+                nc.scalar.copy(out=grouped[:, bt, :, :], in_=gated_planes[(cb, bt)][:].rearrange("p t b -> p b t"))
+            gated_grouped[cb] = grouped
+
+        def quantise_gated(cb):
+            nc.vector.quantize_mx(
+                out=gated_codes[:, cb, :].bitcast(FP8X4),
+                scales=gated_scales[:, cb, :],
+                in_=gated_grouped[cb][:].rearrange("p a b t -> p (a b t)"),
+            )
+
+        gate_stages = (add_bias, squash, mask_and_turn, collect, quantise_gated)
 
         load_activations(0)
         for r in range(LOAD_AHEAD):
             load_raw(r)
-        for g in range(ACT_LEAD):
-            prepare_activations(g)
-        for j in range(BLOCKS + LAG):
-            if j < BLOCKS:
-                r = j // BLOCKS_PER_RAW
-                if j % BLOCKS_PER_RAW == 0:
-                    if r + LOAD_AHEAD < RAW_TILES:
-                        load_raw(r + LOAD_AHEAD)
-                    if r + ACT_LEAD < PASSES:
-                        prepare_activations(r + ACT_LEAD)
-                regroup(j)
-            if j >= LAG:
-                finish(j - LAG)
+        for step in range(-TURN_LEAD * BLOCKS_PER_RAW, BLOCKS + LAG + len(gate_stages)):
+            r, i = divmod(step, BLOCKS_PER_RAW)
+            if i == 0 and 0 <= r + COLLECT_LEAD < PASSES:
+                collect_activations(r + COLLECT_LEAD)
+            if i == 1 and 0 <= r + TURN_LEAD < PASSES:
+                turn_activations(r + TURN_LEAD)
+            if 0 <= step < BLOCKS:
+                if i == 0 and r + LOAD_AHEAD < RAW_TILES:
+                    load_raw(r + LOAD_AHEAD)
+                regroup(step)
+            if i == 2 and 0 <= r + COLLECT_LEAD < PASSES:
+                quantise_activations(r + COLLECT_LEAD)
+            if LAG <= step < BLOCKS + LAG:
+                finish(step - LAG)
+            for n in range(len(gate_stages)):
+                cb, i_done = divmod(step - LAG - n - 1 - FIRST_MEMORY_BLOCK, BLOCKS_PER_RAW)
+                if 0 <= cb < COL_BLOCKS and i_done == BLOCKS_PER_RAW - 1:
+                    gate_stages[n](cb)
 
+        out_sums = [sums.tile([P, H], F32, tag="sum", name="out_sum%d" % bt) for bt in range(B_TILES)]
+        for g in range(ME_PASSES):
+            multiply(
+                out_sums, gated_codes[:, g, :], gated_scales[:, g, :], read_codes[:, g, :], read_scales[:, g, :],
+                g == 0, g == ME_PASSES - 1,
+            )
         for bt in range(B_TILES):
-            result = gate_pool.tile([P, H], F32, tag="result", name="result")
+            result = gate_pool.tile([P, H], F32, tag="result", name="result", bufs=2)
             if bt == 0:
                 nc.scalar.copy(out=result[:], in_=out_sums[bt][:])
             else:

@@ -59,7 +59,20 @@ def tile_lstmcell_pa_k_kernel(tc, x, me_output, W_memi, W_memh, W_memt, mem_bias
         nc.vector.memset(warm[:], 0.0)
         nc.scalar.activation(out=warm[:], in_=warm[:], func=SIGMOID)
 
+        bias_row = const.tile([1, OH], BF16)
+        nc.sync.dma_start(out=bias_row[:], in_=mem_bias.rearrange("(o n) -> o n", o=1))
+        ones = const.tile([P, P], BF16)
+        nc.vector.memset(ones[:], 1.0)
+        bias_rows = const.tile([P, OH], BF16)
+        nc.vector.memset(bias_rows[:], 0.0)
+        nc.vector.tensor_copy(out=bias_rows[0:1, :], in_=bias_row[:])
         bias_all = const.tile([P, OH], BF16)
+        for cb in range(COL_BLOCKS):
+            cols = slice(cb * N_BLOCK, (cb + 1) * N_BLOCK)
+            spread = turn.tile([P, N_BLOCK], F32, tag="turn", name="spread")
+            nc.tensor.matmul(out=spread[:], lhsT=ones[:], rhs=bias_rows[:, cols], start=True, stop=True)
+            nc.vector.tensor_copy(out=bias_all[:, cols], in_=spread[:])
+
         act_codes = const.tile([P, PASSES, B], U32, align_bytes=64)
         act_scales = const.tile([P, PASSES, B], U8, align_bytes=64)
         gated_codes = const.tile([P, ME_PASSES, B], U32, align_bytes=64)
@@ -89,8 +102,6 @@ def tile_lstmcell_pa_k_kernel(tc, x, me_output, W_memi, W_memh, W_memt, mem_bias
                     x_slabs[s].append(slab)
                 else:
                     nc.sync.dma_start(out=me_rows[bt][:], in_=me_output[rows, :])
-            if s == X_SLABS:
-                nc.sync.dma_start(out=bias_all[:], in_=mem_bias.partition_broadcast(P))
 
         def load_raw(r):
             if r + SLAB_LEAD < PASSES and (r + SLAB_LEAD) % SLAB_PASSES == 0:
@@ -115,10 +126,11 @@ def tile_lstmcell_pa_k_kernel(tc, x, me_output, W_memi, W_memh, W_memt, mem_bias
                         ),
                     )
             else:
-                nc.sync.dma_start(
-                    out=raw[:].rearrange("p (gt c) -> p gt c", c=N_BLOCK),
-                    in_=W_memt.rearrange("(gt p) c -> p gt c", p=P),
-                )
+                for g in range(ME_PASSES):
+                    nc.sync.dma_start(
+                        out=raw[:].rearrange("p (g t c) -> p g t c", t=PACK, c=N_BLOCK)[:, g, :, :],
+                        in_=W_memt[g * K_PASS : (g + 1) * K_PASS, :].rearrange("(t p) c -> p t c", p=P),
+                    )
             raw_tiles.append(raw)
 
         def block_source(r, i):

@@ -48,7 +48,6 @@ def tile_lstmcell_pa_k_kernel(tc, x, me_output, W_memi, W_memh, W_memt, mem_bias
         tc.tile_pool(name="gate", bufs=4) as gate_pool,
         tc.psum_pool(name="sums", bufs=B_TILES * COL_BLOCKS) as sums,
         tc.psum_pool(name="turn", bufs=2) as turn,
-        tc.manual_schedule(),
     ):
         ident_f32 = const.tile([P, P], F32)
         make_identity(nc, ident_f32[:])

import concourse.mybir as mybir
from concourse.masks import make_identity

F32 = mybir.dt.float32
BF16 = mybir.dt.bfloat16
U32 = mybir.dt.uint32
U8 = mybir.dt.uint8
FP8X4 = mybir.dt.float8_e4m3fn_x4
ADD = mybir.AluOpType.add
MULT = mybir.AluOpType.mult
SIGMOID = mybir.ActivationFunctionType.Sigmoid

B, I, OH, H = 256, 8192, 1536, 512
FLOPS = 2 * B * (I * OH + OH * OH + OH * H)

P = 128
PACK = 4
K_PASS = P * PACK
N_BLOCK = 512
B_TILES = B // P

X_PASSES = I // K_PASS
ME_PASSES = OH // K_PASS
PASSES = X_PASSES + ME_PASSES
COL_BLOCKS = OH // N_BLOCK

BLOCKS_PER_RAW = 3
RAW_TILES = X_PASSES + COL_BLOCKS + 1
BLOCKS = RAW_TILES * BLOCKS_PER_RAW
FIRST_MEMORY_BLOCK = X_PASSES * BLOCKS_PER_RAW

SLAB_PASSES = 4
X_SLABS = X_PASSES // SLAB_PASSES
LOAD_AHEAD = 5
TURN_LEAD = 4
COLLECT_LEAD = 2
SLAB_LEAD = 3
LAG = 2


def tile_lstmcell_pa_k_kernel(tc, x, me_output, W_memi, W_memh, W_memt, mem_bias, out):
    nc = tc.nc
    with (
        tc.tile_pool(name="const", bufs=1) as const,
        tc.tile_pool(name="slabs", bufs=3) as slabs,
        tc.tile_pool(name="raws", bufs=LOAD_AHEAD + 1) as raws,
        tc.tile_pool(name="stream", bufs=6) as stream,
        tc.tile_pool(name="gate", bufs=4) as gate_pool,
        tc.psum_pool(name="sums", bufs=B_TILES * COL_BLOCKS) as sums,
        tc.psum_pool(name="turn", bufs=2) as turn,
    ):
        ident_f32 = const.tile([P, P], F32)
        make_identity(nc, ident_f32[:])
        ident_bf16 = const.tile([P, P], BF16)
        make_identity(nc, ident_bf16[:])

        warm = const.tile([P, 1], F32)
        nc.vector.memset(warm[:], 0.0)
        nc.scalar.activation(out=warm[:], in_=warm[:], func=SIGMOID)

        bias_row = const.tile([1, OH], BF16)
        nc.sync.dma_start(out=bias_row[:], in_=mem_bias.rearrange("(o n) -> o n", o=1))
        ones = const.tile([P, P], BF16)
        nc.vector.memset(ones[:], 1.0)
        bias_rows = const.tile([P, OH], BF16)
        nc.vector.memset(bias_rows[:], 0.0)
        nc.vector.tensor_copy(out=bias_rows[0:1, :], in_=bias_row[:])
        bias_all = const.tile([P, OH], BF16)
        for cb in range(COL_BLOCKS):
            cols = slice(cb * N_BLOCK, (cb + 1) * N_BLOCK)
            spread = turn.tile([P, N_BLOCK], F32, tag="turn", name="spread")
            nc.tensor.matmul(out=spread[:], lhsT=ones[:], rhs=bias_rows[:, cols], start=True, stop=True)
            nc.vector.tensor_copy(out=bias_all[:, cols], in_=spread[:])

        act_codes = const.tile([P, PASSES, B], U32, align_bytes=64)
        act_scales = const.tile([P, PASSES, B], U8, align_bytes=64)
        gated_codes = const.tile([P, ME_PASSES, B], U32, align_bytes=64)
        gated_scales = const.tile([P, ME_PASSES, B], U8, align_bytes=64)
        read_codes = const.tile([P, ME_PASSES, H], U32, align_bytes=64)
        read_scales = const.tile([P, ME_PASSES, H], U8, align_bytes=64)
        me_rows = [const.tile([P, OH], BF16, name="me_rows%d" % bt) for bt in range(B_TILES)]
        x_slabs = []
        raw_tiles = []
        grouped_tiles = []
        turned = {}
        act_grouped = {}
        mg = [
            [sums.tile([P, N_BLOCK], F32, tag="sum", name="mg%d_%d" % (bt, cb)) for cb in range(COL_BLOCKS)]
            for bt in range(B_TILES)
        ]

        def load_activations(s):
            for bt in range(B_TILES):
                rows = slice(bt * P, (bt + 1) * P)
                if s < X_SLABS:
                    if bt == 0:
                        x_slabs.append([])
                    slab = slabs.tile([P, SLAB_PASSES * K_PASS], BF16, tag="slab%d" % bt, name="slab%d" % bt)
                    width = SLAB_PASSES * K_PASS
                    nc.sync.dma_start(out=slab[:], in_=x[rows, s * width : (s + 1) * width])
                    x_slabs[s].append(slab)
                else:
                    nc.sync.dma_start(out=me_rows[bt][:], in_=me_output[rows, :])

        def load_raw(r):
            if r + SLAB_LEAD < PASSES and (r + SLAB_LEAD) % SLAB_PASSES == 0:
                load_activations((r + SLAB_LEAD) // SLAB_PASSES)
            raw = raws.tile([P, BLOCKS_PER_RAW * PACK * N_BLOCK], BF16, tag="raw", name="raw")
            if r < X_PASSES:
                rows_of_pass = W_memi[r * K_PASS : (r + 1) * K_PASS, :].rearrange("(q t) c -> q t c", t=PACK)
                pieces = BLOCKS_PER_RAW if r == 0 else 1
                width = OH // pieces
                for piece in range(pieces):
                    cols = slice(piece * width, (piece + 1) * width)
                    nc.sync.dma_start(
                        out=raw[:].rearrange("q (t c) -> q t c", t=PACK)[:, :, cols], in_=rows_of_pass[:, :, cols]
                    )
            elif r < X_PASSES + COL_BLOCKS:
                cb = r - X_PASSES
                for g in range(ME_PASSES):
                    nc.sync.dma_start(
                        out=raw[:].rearrange("q (g t c) -> q g t c", t=PACK, c=N_BLOCK)[:, g, :, :],
                        in_=W_memh[g * K_PASS : (g + 1) * K_PASS, cb * N_BLOCK : (cb + 1) * N_BLOCK].rearrange(
                            "(q t) c -> q t c", t=PACK
                        ),
                    )
            else:
                for g in range(ME_PASSES):
                    nc.sync.dma_start(
                        out=raw[:].rearrange("p (g t c) -> p g t c", t=PACK, c=N_BLOCK)[:, g, :, :],
                        in_=W_memt[g * K_PASS : (g + 1) * K_PASS, :].rearrange("(t p) c -> p t c", p=P),
                    )
            raw_tiles.append(raw)

        def block_source(r, i):
            if r < X_PASSES:
                return raw_tiles[r][:].rearrange("q (t c) -> q t c", t=PACK)[:, :, i * N_BLOCK : (i + 1) * N_BLOCK]
            return raw_tiles[r][:].rearrange("p (g t c) -> p g t c", t=PACK, c=N_BLOCK)[:, i, :, :]

        def turn_activations(g):
            if g < X_PASSES:
                row_tiles, local = x_slabs[g // SLAB_PASSES], g % SLAB_PASSES
            else:
                row_tiles, local = me_rows, g - X_PASSES
            words = turn.tile([P, B_TILES, 2, P], F32, tag="turn", name="words")
            for bt in range(B_TILES):
                as_words = row_tiles[bt][:].bitcast(F32).rearrange("b (q u) -> b q u", u=2)
                for u in range(2):
                    nc.tensor.transpose(words[:, bt, u, :], as_words[:, local * P : (local + 1) * P, u], ident_f32[:])
            turned[g] = words

        def collect_activations(g):
            grouped = stream.tile([P, B_TILES, P, PACK], BF16, tag="act_grouped", name="act_grouped", bufs=3, align_bytes=64)
            nc.scalar.copy(out=grouped[:].bitcast(F32), in_=turned[g][:].rearrange("q a u b -> q a b u"))
            act_grouped[g] = grouped

        def quantise_activations(g):
            nc.vector.quantize_mx(
                out=act_codes[:, g, :].bitcast(FP8X4),
                scales=act_scales[:, g, :],
                in_=act_grouped[g][:].rearrange("p a b t -> p (a b t)"),
            )

        def regroup(j):
            source = block_source(j // BLOCKS_PER_RAW, j % BLOCKS_PER_RAW)
            grouped = stream.tile([P, N_BLOCK, PACK], BF16, tag="grouped", name="grouped", bufs=8, align_bytes=64)
            dst = grouped[:].rearrange("p (c i) t -> p c t i", i=4)
            src = source.rearrange("p t (c i) -> p c t i", i=4)
            if j % 2 == 0:
                nc.vector.tensor_copy(out=dst, in_=src)
            else:
                nc.scalar.copy(out=dst, in_=src)
            grouped_tiles.append(grouped)

        def multiply(sum_tiles, codes_of_pass, scales_of_pass, codes, scales, start, stop):
            for bt in range(B_TILES):
                rows = slice(bt * P, (bt + 1) * P)
                nc.tensor.matmul_mx(
                    out=sum_tiles[bt][:],
                    lhsT=codes_of_pass[:, rows].bitcast(FP8X4),
                    lhsT_scale=scales_of_pass[:, rows],
                    rhs=codes.bitcast(FP8X4),
                    rhs_scale=scales,
                    start=start,
                    stop=stop,
                )

        def finish(j):
            r, i = divmod(j, BLOCKS_PER_RAW)
            if r < X_PASSES + COL_BLOCKS:
                codes = stream.tile([P, N_BLOCK], U32, tag="codes", name="codes", align_bytes=64)[:]
                scales = stream.tile([P, N_BLOCK], U8, tag="scales", name="scales", align_bytes=64)[:]
            else:
                codes = read_codes[:, i, :]
                scales = read_scales[:, i, :]
            nc.vector.quantize_mx(
                out=codes.bitcast(FP8X4), scales=scales, in_=grouped_tiles[j][:].rearrange("p c t -> p (c t)")
            )
            if r < X_PASSES:
                column = [mg[bt][i] for bt in range(B_TILES)]
                multiply(column, act_codes[:, r, :], act_scales[:, r, :], codes, scales, r == 0, False)
            elif r < X_PASSES + COL_BLOCKS:
                cb = r - X_PASSES
                g = X_PASSES + i
                column = [mg[bt][cb] for bt in range(B_TILES)]
                multiply(column, act_codes[:, g, :], act_scales[:, g, :], codes, scales, False, i == ME_PASSES - 1)

        z_tiles = {}
        gated_planes = {}
        gated_grouped = {}

        def add_bias(cb):
            cols = slice(cb * N_BLOCK, (cb + 1) * N_BLOCK)
            for bt in range(B_TILES):
                z = gate_pool.tile([P, N_BLOCK], F32, tag="z", name="z")
                nc.vector.tensor_tensor(out=z[:], in0=mg[bt][cb][:], in1=bias_all[:, cols], op=ADD)
                z_tiles[(cb, bt)] = z

        def squash(cb):
            for bt in range(B_TILES):
                z = z_tiles[(cb, bt)]
                nc.scalar.activation(out=z[:], in_=z[:], func=SIGMOID)

        def mask_and_turn(cb):
            cols = slice(cb * N_BLOCK, (cb + 1) * N_BLOCK)
            for bt in range(B_TILES):
                gated = gate_pool.tile([P, N_BLOCK], BF16, tag="gated", name="gated")
                nc.vector.tensor_tensor(out=gated[:], in0=z_tiles[(cb, bt)][:], in1=me_rows[bt][:, cols], op=MULT)
                planes = turn.tile([P, PACK, P], BF16, tag="turn", name="planes")
                for t in range(PACK):
                    nc.tensor.transpose(planes[:, t, :], gated[:, t * P : (t + 1) * P], ident_bf16[:])
                gated_planes[(cb, bt)] = planes

        def collect(cb):
            grouped = gate_pool.tile([P, B_TILES, P, PACK], BF16, tag="gated_grouped", name="gated_grouped", bufs=2, align_bytes=64)
            for bt in range(B_TILES):
                nc.scalar.copy(out=grouped[:, bt, :, :], in_=gated_planes[(cb, bt)][:].rearrange("p t b -> p b t"))
            gated_grouped[cb] = grouped

        def quantise_gated(cb):
            nc.vector.quantize_mx(
                out=gated_codes[:, cb, :].bitcast(FP8X4),
                scales=gated_scales[:, cb, :],
                in_=gated_grouped[cb][:].rearrange("p a b t -> p (a b t)"),
            )

        gate_stages = (add_bias, squash, mask_and_turn, collect, quantise_gated)

        load_activations(0)
        for r in range(LOAD_AHEAD):
            load_raw(r)
        for step in range(-TURN_LEAD * BLOCKS_PER_RAW, BLOCKS + LAG + len(gate_stages)):
            r, i = divmod(step, BLOCKS_PER_RAW)
            if i == 0 and 0 <= r + COLLECT_LEAD < PASSES:
                collect_activations(r + COLLECT_LEAD)
            if i == 1 and 0 <= r + TURN_LEAD < PASSES:
                turn_activations(r + TURN_LEAD)
            if 0 <= step < BLOCKS:
                if i == 0 and r + LOAD_AHEAD < RAW_TILES:
                    load_raw(r + LOAD_AHEAD)
                regroup(step)
            if i == 2 and 0 <= r + COLLECT_LEAD < PASSES:
                quantise_activations(r + COLLECT_LEAD)
            if LAG <= step < BLOCKS + LAG:
                finish(step - LAG)
            for n in range(len(gate_stages)):
                cb, i_done = divmod(step - LAG - n - 1 - FIRST_MEMORY_BLOCK, BLOCKS_PER_RAW)
                if 0 <= cb < COL_BLOCKS and i_done == BLOCKS_PER_RAW - 1:
                    gate_stages[n](cb)

        out_sums = [sums.tile([P, H], F32, tag="sum", name="out_sum%d" % bt) for bt in range(B_TILES)]
        for g in range(ME_PASSES):
            multiply(
                out_sums, gated_codes[:, g, :], gated_scales[:, g, :], read_codes[:, g, :], read_scales[:, g, :],
                g == 0, g == ME_PASSES - 1,
            )
        for bt in range(B_TILES):
            result = gate_pool.tile([P, H], F32, tag="result", name="result", bufs=2)
            if bt == 0:
                nc.scalar.copy(out=result[:], in_=out_sums[bt][:])
            else:
                nc.vector.tensor_copy(out=result[:], in_=out_sums[bt][:])
            nc.sync.dma_start(out=out[bt * P : (bt + 1) * P, :], in_=result[:])
